import numpy as np
import ml_dtypes


def mxq(x, axis, fmt="e4m3"):
    dtype, down = {"e4m3": (ml_dtypes.float8_e4m3fn, 7), "e5m2": (ml_dtypes.float8_e5m2, 14)}[fmt]
    v = np.moveaxis(np.asarray(x, np.float32).astype(ml_dtypes.bfloat16).astype(np.float64), axis, -1)
    blocks = v.reshape(v.shape[:-1] + (-1, 32))
    amax = np.abs(blocks).max(-1, keepdims=True)
    byte = np.maximum(np.where(amax > 0, np.frexp(amax)[1] - 1 + 127, 0) - down, 1)
    scale = np.exp2(byte - 127.0)
    codes = (blocks / scale).astype(np.float32).astype(dtype).astype(np.float64)
    return np.moveaxis((codes * scale).reshape(v.shape), -1, axis)


WIDE = False


def mx_kscale(k):
    if not WIDE:
        return np.ones(k)
    levels = np.array([10, -10, 5, -5, 0])
    if k % 512:
        return np.exp2(np.random.permutation(np.resize(levels, k // 32))).repeat(32)
    a = np.empty((k // 512, 16))
    for p in range(k // 512):
        a[p, :8] = np.random.permutation(np.resize(levels, 8))
        for g in range(8):
            far = levels[np.abs(levels - a[p, g]) >= 10]
            a[p, g + 8] = far[np.random.randint(len(far))]
    return np.exp2(a.ravel()).repeat(32)


BF16 = ml_dtypes.bfloat16


def bf(x):
    return np.asarray(x, np.float32).astype(BF16)


def f64(x):
    return np.asarray(x).astype(np.float64)


B, D_IN, H, D_OUT = 8192, 4096, 512, 128
H2 = 2 * H
LN_EPS = 1e-5


def draw0():
    s = mx_kscale(H)
    t = mx_kscale(H2)
    return {
        "h1": bf(np.tanh(np.random.standard_normal((B, H))) * s),
        "W_ih1": bf(np.random.standard_normal((H, H)) / np.sqrt(H) / s[None, :]),
        "b_ih1": bf(0.25 + 0.3 * np.random.standard_normal(H)),
        "b_hh1": bf(0.3 * np.random.standard_normal(H)),
        "ln_g": bf((1.0 + 0.1 * np.random.standard_normal(H2)) * t),
        "ln_b": bf(0.2 * np.random.standard_normal(H2) * t),
        "fc_W": bf(np.random.standard_normal((D_OUT, H2)) / np.sqrt(H2) / t[None, :]),
        "fc_b": bf(0.3 * np.random.standard_normal(D_OUT)),
    }


def core(h1, W_ih1, b_ih1, b_hh1, ln_g, ln_b, fc_W, fc_b):
    h2 = np.tanh((mxq(f64(h1), 1, "e4m3") @ mxq(f64(W_ih1), 1, "e4m3").T) + f64(b_ih1) + f64(b_hh1))
    combined = np.concatenate([h2, h2], axis=1)
    mu = combined.mean(axis=-1, keepdims=True)
    var = combined.var(axis=-1, keepdims=True)
    normed = (combined - mu) / np.sqrt(var + LN_EPS) * f64(ln_g) + f64(ln_b)
    return (mxq(normed, 1, "e4m3") @ mxq(f64(fc_W), 1, "e4m3").T) + f64(fc_b)


def e4m3fn_bytes(y):
    return np.clip(np.asarray(y, np.float64), -448.0, 448.0).astype(np.float32).astype(ml_dtypes.float8_e4m3fn).view(np.uint8)


def e4m3fn_values(b):
    return np.asarray(b, np.uint8).view(ml_dtypes.float8_e4m3fn).astype(np.float64)


def setup_inputs():
    d = draw0()
    x0 = np.asarray(d['h1']).astype(np.float64)
    s = (np.max(np.abs(x0), axis=(0,), keepdims=True) / 448.0).astype(np.float32)
    out = {}
    for k, v in d.items():
        if k == 'h1':
            out['h1_bytes'] = e4m3fn_bytes(x0 / s.astype(np.float64))
            out['h1_scale'] = s
        else:
            out[k] = v
    return out


def reference(h1_bytes, h1_scale, W_ih1, b_ih1, b_hh1, ln_g, ln_b, fc_W, fc_b):
    return core(e4m3fn_values(h1_bytes) * h1_scale.astype(np.float64), W_ih1, b_ih1, b_hh1, ln_g, ln_b, fc_W, fc_b)

@@ -1,0 +1,335 @@
+from contextlib import ExitStack
+
+import concourse.mybir as mybir
+from concourse.masks import make_identity
+
+B, H, H2, D_OUT = 8192, 512, 1024, 128
+P = 128
+T = 4
+J = 4
+CH = J * P
+NCH = B // CH
+EPS = 1e-5
+FLOPS = 2 * B * H * H + 2 * B * H2 * D_OUT
+
+F32 = mybir.dt.float32
+BF16 = mybir.dt.bfloat16
+U32 = mybir.dt.uint32
+U8 = mybir.dt.uint8
+FP8 = mybir.dt.float8_e4m3fn
+FP8X4 = mybir.dt.float8_e4m3fn_x4
+ACT = mybir.ActivationFunctionType
+ALU = mybir.AluOpType
+
+
+def tile_rnnclassifier_pa_t_kernel(tc, h1_bytes, h1_scale, W_ih1, b_ih1, b_hh1, ln_g, ln_b, fc_W, fc_b, out):
+    nc = tc.nc
+    x_view = h1_bytes.rearrange("(c q j) k -> c q j k", q=P, j=J)
+    out_view = out.rearrange("(c q j) f -> c q j f", q=P, j=J)
+
+    with ExitStack() as ctx:
+        const = ctx.enter_context(tc.tile_pool(name="const", bufs=1))
+        loads = ctx.enter_context(tc.tile_pool(name="loads", bufs=3))
+        work = ctx.enter_context(tc.tile_pool(name="work", bufs=2))
+        stat = ctx.enter_context(tc.tile_pool(name="stat", bufs=3))
+        ps_m = ctx.enter_context(tc.psum_pool(name="ps_m", bufs=1))
+        ps_s = ctx.enter_context(tc.psum_pool(name="ps_s", bufs=2))
+        ps_t = ctx.enter_context(tc.psum_pool(name="ps_t", bufs=1))
+        ps_q = ctx.enter_context(tc.psum_pool(name="ps_q", bufs=2))
+        ps_f = ctx.enter_context(tc.psum_pool(name="ps_f", bufs=2))
+
+        xb, hx, xg, xc, xs = {}, {}, {}, {}, {}
+        hh, zz, mv, rs, nb = {}, {}, {}, {}, {}
+        yy, yg, yc, ys = {}, {}, {}, {}
+        tmb, tqb, fmb, xtb, s1b, ob, st = {}, {}, {}, {}, {}, {}, {}
+
+        def load(c):
+            xb[c] = loads.tile([P, J, H], U8, name="x_bytes", align_bytes=64)
+            nc.sync.dma_start(out=xb[c][:], in_=x_view[c])
+
+        load(0)
+        scale = const.tile([P, 2, H], F32)
+        nc.sync.dma_start(out=scale[:, 0, :], in_=h1_scale.rearrange("o k -> (o k)").partition_broadcast(P))
+        w_sb = const.tile([P, T, H], BF16)
+        nc.sync.dma_start(out=w_sb[:], in_=W_ih1.rearrange("(m t) k -> m t k", t=T))
+        load(1)
+        f_sb = const.tile([P, H2], BF16)
+        nc.sync.dma_start(out=f_sb[:], in_=fc_W)
+        b1 = const.tile([P, T], BF16)
+        nc.gpsimd.dma_start(out=b1[:], in_=b_ih1.rearrange("(p t) -> p t", t=T))
+        b2 = const.tile([P, T], BF16)
+        nc.gpsimd.dma_start(out=b2[:], in_=b_hh1.rearrange("(p t) -> p t", t=T))
+        g_raw = const.tile([P, 2, T], BF16)
+        nc.gpsimd.dma_start(out=g_raw[:], in_=ln_g.rearrange("(o p t) -> p o t", o=2, t=T))
+        b_raw = const.tile([P, 2, T], BF16)
+        nc.gpsimd.dma_start(out=b_raw[:], in_=ln_b.rearrange("(o p t) -> p o t", o=2, t=T))
+        fcb_raw = const.tile([P, D_OUT], BF16)
+        nc.gpsimd.dma_start(out=fcb_raw[:], in_=fc_b.partition_broadcast(P))
+
+        ident = const.tile([P, P], F32)
+        make_identity(nc, ident[:])
+        half = const.tile([P, 4], F32)
+        nc.gpsimd.memset(half[:], -0.5)
+        dummy = const.tile([P, 1], F32)
+        nc.gpsimd.memset(dummy[:], 0.0)
+        nc.scalar.activation(out=dummy[:], in_=dummy[:], func=ACT.Tanh)
+
+        nc.vector.tensor_copy(out=scale[:, 1, :], in_=scale[:, 0, :])
+        bsum = const.tile([P, T], F32)
+        g_col = const.tile([P, 2, T], F32)
+        b_col = const.tile([P, 2, T], F32)
+        fcb = const.tile([P, J, D_OUT], F32)
+
+        w_grp = const.tile([P, H, T], BF16, align_bytes=64)
+        w_codes = const.tile([P, H], U32, align_bytes=64)
+        w_scales = const.tile([P, H], U8, align_bytes=64)
+        f_grp = const.tile([P, 2 * D_OUT, T], BF16, align_bytes=64)
+        f_codes = const.tile([P, 2 * D_OUT], U32, align_bytes=64)
+        f_scales = const.tile([P, 2 * D_OUT], U8, align_bytes=64)
+
+        def words(ap):
+            return ap.bitcast(F32)
+
+        def a1(c, h):
+            if h == 0:
+                hx[c] = work.tile([P, J, H], BF16, name="hx", align_bytes=64, bufs=2)
+            dst = hx[c][:, 2 * h : 2 * h + 2, :].rearrange("p j k -> p (j k)")
+            code = xb[c][:, 2 * h : 2 * h + 2, :].rearrange("p j k -> p (j k)").bitcast(FP8)
+            nc.vector.tensor_tensor(out=dst, in0=code, in1=scale[:].rearrange("p a k -> p (a k)"), op=ALU.mult)
+
+        def a2p(c, h):
+            xtb[c, h] = ps_m.tile([P, 2, 2, P], F32, name="misc")
+            for jj in range(2):
+                w = words(hx[c][:, 2 * h + jj, :])
+                for u in range(2):
+                    nc.tensor.transpose(xtb[c, h][:, jj, u, :], w[:, u : H // 2 : 2], ident[:])
+
+        def a2s(c, h):
+            if h == 0:
+                xg[c] = work.tile([P, CH, T], BF16, name="xg", align_bytes=64, bufs=2)
+            dst = words(xg[c][:, h * 256 : h * 256 + 256, :]).rearrange("p (j r) u -> p j r u", j=2)
+            nc.scalar.copy(out=dst, in_=xtb[c, h][:].rearrange("p j u r -> p j r u"))
+
+        def a3(c):
+            xc[c] = work.tile([P, CH], U32, name="xc", align_bytes=64)
+            xs[c] = work.tile([P, CH], U8, name="xs", align_bytes=64)
+            nc.vector.quantize_mx(out=xc[c][:].bitcast(FP8X4), scales=xs[c][:], in_=xg[c][:].rearrange("p n t -> p (n t)"))
+
+        def bp(c, t):
+            s1b[c, t] = ps_s.tile([P, CH], F32, name="s1")
+            nc.tensor.matmul_mx(
+                out=s1b[c, t][:],
+                lhsT=w_codes[:, t * P : (t + 1) * P].bitcast(FP8X4),
+                lhsT_scale=w_scales[:, t * P : (t + 1) * P],
+                rhs=xc[c][:].bitcast(FP8X4),
+                rhs_scale=xs[c][:],
+                start=True,
+                stop=True,
+            )
+
+        def bs(c, t):
+            if c not in hh:
+                hh[c] = work.tile([P, T, CH], F32, name="hh", bufs=3)
+            nc.scalar.activation(out=hh[c][:, t, :], in_=s1b[c, t][:], func=ACT.Tanh, bias=bsum[:, t : t + 1])
+
+        def cp(c, j):
+            tmb[c, j] = ps_t.tile([P, T, P], F32, name="tm")
+            for t in range(T):
+                nc.tensor.transpose(tmb[c, j][:, t, :], hh[c][:, t, j * P : (j + 1) * P], ident[:])
+
+        def cq(c, j):
+            tqb[c, j] = ps_q.tile([P, T, P], F32, name="tq")
+            for t in range(T):
+                nc.tensor.transpose(tqb[c, j][:, t, :], hh[c][:, t, j * P : (j + 1) * P], ident[:])
+
+        def cv(c, j):
+            if c not in mv:
+                mv[c] = stat.tile([P, J, 2], F32, name="mv")
+                rs[c] = stat.tile([P, J], F32, name="rs")
+                nb[c] = stat.tile([P, J], F32, name="nb")
+                st[c] = stat.tile([P, J, 6], F32, name="st")
+            nc.vector.bn_stats(out=st[c][:, j, :], in_=tmb[c, j][:].rearrange("p t m -> p (t m)"))
+
+        def ca(c, j):
+            nc.vector.bn_aggr(out=mv[c][:, j, :], in_=st[c][:, j, :])
+
+        def cg(c, j):
+            if j % 4 != 3:
+                return
+            js = slice(j - 3, j + 1)
+            nc.gpsimd.tensor_scalar(out=rs[c][:, js], in0=mv[c][:, js, 1], scalar1=EPS, scalar2=None, op0=ALU.add)
+            nc.gpsimd.tensor_scalar(out=nb[c][:, js], in0=mv[c][:, js, 0], scalar1=-1.0, scalar2=None, op0=ALU.mult)
+            nc.gpsimd.tensor_tensor(out=rs[c][:, js], in0=rs[c][:, js], in1=half[:], op=ALU.pow)
+            nc.gpsimd.tensor_tensor(out=nb[c][:, js], in0=nb[c][:, js], in1=rs[c][:, js], op=ALU.mult)
+
+        def cs(c, j):
+            if c not in zz:
+                zz[c] = work.tile([P, J, H], F32, name="zz", bufs=2)
+            src = tqb[c, j][:].rearrange("p t m -> p (t m)")
+            if j in []:
+                nc.vector.tensor_scalar(
+                    out=zz[c][:, j, :], in0=src, scalar1=rs[c][:, j : j + 1], scalar2=nb[c][:, j : j + 1], op0=ALU.mult, op1=ALU.add
+                )
+            else:
+                nc.scalar.activation(out=zz[c][:, j, :], in_=src, func=ACT.Identity, scale=rs[c][:, j : j + 1], bias=nb[c][:, j : j + 1])
+
+        def dp(c, t):
+            fmb[c, t] = ps_f.tile([P, CH], F32, name="fm")
+            for j in range(J):
+                nc.tensor.transpose(fmb[c, t][:, j * P : (j + 1) * P], zz[c][:, j, t * P : (t + 1) * P], ident[:])
+
+        def ds(c, t, o):
+            if (c, o) not in yy:
+                yy[c, o] = work.tile([P, T, CH], BF16, name="yy%d" % o, bufs=2)
+            if 2 * t + o in []:
+                nc.vector.tensor_scalar(
+                    out=yy[c, o][:, t, :], in0=fmb[c, t][:], scalar1=g_col[:, o, t : t + 1], scalar2=b_col[:, o, t : t + 1], op0=ALU.mult, op1=ALU.add
+                )
+            else:
+                nc.scalar.activation(
+                    out=yy[c, o][:, t, :], in_=fmb[c, t][:], func=ACT.Identity, scale=g_col[:, o, t : t + 1], bias=b_col[:, o, t : t + 1]
+                )
+
+        def e1(c, o, part):
+            if (c, o) not in yg:
+                yg[c, o] = work.tile([P, CH, T], BF16, name="yg%d" % o, align_bytes=64, bufs=2)
+            if 2 * o + part in []:
+                for q in range(2):
+                    ns = slice(256 * part + 128 * q, 256 * part + 128 * q + 128)
+                    nc.gpsimd.tensor_scalar(
+                        out=yg[c, o][:, ns, :], in0=yy[c, o][:, :, ns].rearrange("p t n -> p n t"), scalar1=1.0, scalar2=0.0, op0=ALU.mult, op1=ALU.add
+                    )
+            else:
+                ns = slice(256 * part, 256 * part + 256)
+                nc.vector.tensor_copy(
+                    out=yg[c, o][:, ns, :].rearrange("p (n i) t -> p n t i", i=4),
+                    in_=yy[c, o][:, :, ns].rearrange("p t (n i) -> p n t i", i=4),
+                )
+
+        def e2(c, o):
+            yc[c, o] = work.tile([P, CH], U32, name="yc%d" % o, align_bytes=64)
+            ys[c, o] = work.tile([P, CH], U8, name="ys%d" % o, align_bytes=64)
+            nc.vector.quantize_mx(out=yc[c, o][:].bitcast(FP8X4), scales=ys[c, o][:], in_=yg[c, o][:].rearrange("p n t -> p (n t)"))
+
+        def fp(c):
+            ob[c] = ps_m.tile([P, J, D_OUT], F32, name="misc")
+            for j in range(J):
+                for o in range(2):
+                    nc.tensor.matmul_mx(
+                        out=ob[c][:, j, :],
+                        lhsT=yc[c, o][:, j * P : (j + 1) * P].bitcast(FP8X4),
+                        lhsT_scale=ys[c, o][:, j * P : (j + 1) * P],
+                        rhs=f_codes[:, o * P : (o + 1) * P].bitcast(FP8X4),
+                        rhs_scale=f_scales[:, o * P : (o + 1) * P],
+                        start=(o == 0),
+                        stop=(o == 1),
+                    )
+
+        def fv(c):
+            osb = work.tile([P, J, D_OUT], F32, name="osb")
+            nc.vector.tensor_tensor(out=osb[:], in0=ob[c][:], in1=fcb[:], op=ALU.add)
+            nc.sync.dma_start(out=out_view[c], in_=osb[:])
+
+        def weights():
+            for h in range(2):
+                xt = ps_m.tile([P, 2, 2, P], F32, name="misc")
+                for tt in range(2):
+                    w = words(w_sb[:, 2 * h + tt, :])
+                    for u in range(2):
+                        nc.tensor.transpose(xt[:, tt, u, :], w[:, u : H // 2 : 2], ident[:])
+                dst = words(w_grp[:, h * 256 : h * 256 + 256, :]).rearrange("p (j r) u -> p j r u", j=2)
+                nc.scalar.copy(out=dst, in_=xt[:].rearrange("p j u r -> p j r u"))
+            nc.vector.quantize_mx(out=w_codes[:].bitcast(FP8X4), scales=w_scales[:], in_=w_grp[:].rearrange("p n t -> p (n t)"))
+
+        def fc_weights():
+            xt = ps_m.tile([P, 2, 2, P], F32, name="misc")
+            w = words(f_sb[:])
+            for o in range(2):
+                for u in range(2):
+                    nc.tensor.transpose(xt[:, o, u, :], w[:, 256 * o + u : 256 * (o + 1) : 2], ident[:])
+            dst = words(f_grp[:]).rearrange("p (j r) u -> p j r u", j=2)
+            nc.scalar.copy(out=dst, in_=xt[:].rearrange("p j u r -> p j r u"))
+            nc.vector.quantize_mx(out=f_codes[:].bitcast(FP8X4), scales=f_scales[:], in_=f_grp[:].rearrange("p n t -> p (n t)"))
+
+        def small_constants():
+            nc.vector.tensor_tensor(out=bsum[:], in0=b1[:], in1=b2[:], op=ALU.add)
+            nc.vector.tensor_copy(out=g_col[:], in_=g_raw[:])
+            nc.vector.tensor_copy(out=b_col[:], in_=b_raw[:])
+            for j in range(J):
+                nc.vector.tensor_copy(out=fcb[:, j, :], in_=fcb_raw[:])
+
+        steps = [
+            (dp, (1,), 3),
+            (e1, (0, 1), 4),
+            (bp, (1,), 1),
+            (ds, (3, 1), 4),
+            (cg, (1,), 5),
+            (ca, (3,), 2),
+            (bp, (3,), 1),
+            (dp, (0,), 3),
+            (ds, (1, 0), 3),
+            (bp, (0,), 1),
+            (bp, (2,), 1),
+            (cq, (1,), 2),
+            (bs, (1,), 1),
+            (bs, (3,), 1),
+            (bs, (0,), 1),
+            (a1, (0,), 0),
+            (a2p, (0,), 0),
+            (bs, (2,), 1),
+            (fv, (), 5),
+            (ds, (0, 1), 3),
+            (cg, (3,), 2),
+            (cp, (0,), 1),
+            (cp, (1,), 1),
+            (cg, (0,), 5),
+            (ds, (1, 1), 3),
+            (e1, (0, 0), 4),
+            (cg, (2,), 4),
+            (e2, (0,), 4),
+            (ds, (0, 0), 3),
+            (cs, (0,), 2),
+            (dp, (2,), 3),
+            (e1, (1, 1), 4),
+            (cs, (1,), 2),
+            (cq, (3,), 2),
+            (cq, (2,), 2),
+            (cv, (0,), 1),
+            (a1, (1,), 0),
+            (a2s, (0,), 0),
+            (cs, (3,), 2),
+            (a2p, (1,), 0),
+            (cs, (2,), 2),
+            (e1, (1, 0), 4),
+            (cp, (2,), 1),
+            (cv, (1,), 1),
+            (e2, (1,), 4),
+            (dp, (3,), 3),
+            (cq, (0,), 1),
+            (a2s, (1,), 0),
+            (ca, (0,), 1),
+            (ca, (1,), 1),
+            (cp, (3,), 1),
+            (ds, (2, 0), 3),
+            (cv, (2,), 1),
+            (ds, (3, 0), 3),
+            (a3, (), 0),
+            (ds, (2, 1), 3),
+            (cv, (3,), 1),
+            (ca, (2,), 1),
+            (fp, (), 4),
+        ]
+        ctx.enter_context(tc.manual_schedule())
+        a1(0, 0)
+        a1(0, 1)
+        weights()
+        for i in range(NCH + 5):
+            if i + 2 < NCH:
+                load(i + 2)
+            for fn, args, lag in steps:
+                c = i - lag
+                if 0 <= c < NCH and not (fn is a1 and c == 0):
+                    fn(c, *args)
+            if i == 0:
+                small_constants()
+                fc_weights()

@@ -41,7 +41,7 @@ def tile_rnnclassifier_pa_t_kernel(tc, h1_bytes, h1_scale, W_ih1, b_ih1, b_hh1, 
         xb, hx, xg, xc, xs = {}, {}, {}, {}, {}
         hh, zz, mv, rs, nb = {}, {}, {}, {}, {}
         yy, yg, yc, ys = {}, {}, {}, {}
-        tmb, tqb, fmb, xtb, s1b, ob, st = {}, {}, {}, {}, {}, {}, {}
+        osb, tmb, tqb, fmb, xtb, s1b, ob, st = {}, {}, {}, {}, {}, {}, {}, {}
 
         def load(c):
             xb[c] = loads.tile([P, J, H], U8, name="x_bytes", align_bytes=64)
@@ -90,6 +90,12 @@ def tile_rnnclassifier_pa_t_kernel(tc, h1_bytes, h1_scale, W_ih1, b_ih1, b_hh1, 
         def words(ap):
             return ap.bitcast(F32)
 
+        def turn(dst, block, as_matmul):
+            if as_matmul:
+                nc.tensor.matmul(dst, lhsT=block, rhs=ident[:], start=True, stop=True)
+            else:
+                nc.tensor.transpose(dst, block, ident[:])
+
         def a1(c, h):
             if h == 0:
                 hx[c] = work.tile([P, J, H], BF16, name="hx", align_bytes=64, bufs=2)
@@ -135,7 +141,7 @@ def tile_rnnclassifier_pa_t_kernel(tc, h1_bytes, h1_scale, W_ih1, b_ih1, b_hh1, 
         def cp(c, j):
             tmb[c, j] = ps_t.tile([P, T, P], F32, name="tm")
             for t in range(T):
-                nc.tensor.transpose(tmb[c, j][:, t, :], hh[c][:, t, j * P : (j + 1) * P], ident[:])
+                turn(tmb[c, j][:, t, :], hh[c][:, t, j * P : (j + 1) * P], t == 0)
 
         def cq(c, j):
             tqb[c, j] = ps_q.tile([P, T, P], F32, name="tq")
@@ -153,13 +159,20 @@ def tile_rnnclassifier_pa_t_kernel(tc, h1_bytes, h1_scale, W_ih1, b_ih1, b_hh1, 
         def ca(c, j):
             nc.vector.bn_aggr(out=mv[c][:, j, :], in_=st[c][:, j, :])
 
-        def cg(c, j):
-            if j % 4 != 3:
-                return
-            js = slice(j - 3, j + 1)
+        def cgA(c, q):
+            js = slice(4 * q, 4 * q + 4)
             nc.gpsimd.tensor_scalar(out=rs[c][:, js], in0=mv[c][:, js, 1], scalar1=EPS, scalar2=None, op0=ALU.add)
+
+        def cgB(c, q):
+            js = slice(4 * q, 4 * q + 4)
             nc.gpsimd.tensor_scalar(out=nb[c][:, js], in0=mv[c][:, js, 0], scalar1=-1.0, scalar2=None, op0=ALU.mult)
+
+        def cgP(c, q):
+            js = slice(4 * q, 4 * q + 4)
             nc.gpsimd.tensor_tensor(out=rs[c][:, js], in0=rs[c][:, js], in1=half[:], op=ALU.pow)
+
+        def cgM(c, q):
+            js = slice(4 * q, 4 * q + 4)
             nc.gpsimd.tensor_tensor(out=nb[c][:, js], in0=nb[c][:, js], in1=rs[c][:, js], op=ALU.mult)
 
         def cs(c, j):
@@ -176,7 +189,7 @@ def tile_rnnclassifier_pa_t_kernel(tc, h1_bytes, h1_scale, W_ih1, b_ih1, b_hh1, 
         def dp(c, t):
             fmb[c, t] = ps_f.tile([P, CH], F32, name="fm")
             for j in range(J):
-                nc.tensor.transpose(fmb[c, t][:, j * P : (j + 1) * P], zz[c][:, j, t * P : (t + 1) * P], ident[:])
+                turn(fmb[c, t][:, j * P : (j + 1) * P], zz[c][:, j, t * P : (t + 1) * P], j == 0)
 
         def ds(c, t, o):
             if (c, o) not in yy:
@@ -226,9 +239,11 @@ def tile_rnnclassifier_pa_t_kernel(tc, h1_bytes, h1_scale, W_ih1, b_ih1, b_hh1, 
                     )
 
         def fv(c):
-            osb = work.tile([P, J, D_OUT], F32, name="osb")
-            nc.vector.tensor_tensor(out=osb[:], in0=ob[c][:], in1=fcb[:], op=ALU.add)
-            nc.sync.dma_start(out=out_view[c], in_=osb[:])
+            osb[c] = work.tile([P, J, D_OUT], F32, name="osb")
+            nc.vector.tensor_tensor(out=osb[c][:], in0=ob[c][:], in1=fcb[:], op=ALU.add)
+
+        def st_out(c):
+            nc.sync.dma_start(out=out_view[c], in_=osb[c][:])
 
         def weights():
             for h in range(2):
@@ -259,77 +274,78 @@ def tile_rnnclassifier_pa_t_kernel(tc, h1_bytes, h1_scale, W_ih1, b_ih1, b_hh1, 
                 nc.vector.tensor_copy(out=fcb[:, j, :], in_=fcb_raw[:])
 
         steps = [
-            (dp, (1,), 3),
-            (e1, (0, 1), 4),
-            (bp, (1,), 1),
-            (ds, (3, 1), 4),
-            (cg, (1,), 5),
-            (ca, (3,), 2),
+            (cv, (2,), 2),
+            (bs, (1,), 1),
+            (bp, (2,), 1),
+            (cq, (2,), 3),
+            (e1, (0, 0), 4),
+            (cq, (3,), 3),
+            (cp, (3,), 2),
+            (load, (), 0),
+            (a1, (0,), 0),
+            (bs, (2,), 1),
+            (ca, (2,), 2),
+            (cv, (3,), 2),
+            (a1, (1,), 0),
+            (cs, (2,), 3),
             (bp, (3,), 1),
+            (cs, (3,), 3),
+            (ds, (3, 1), 4),
+            (bs, (3,), 1),
+            (bp, (0,), 1),
+            (e1, (1, 0), 4),
+            (bs, (0,), 1),
+            (a2p, (0,), 0),
+            (e1, (1, 1), 4),
+            (dp, (1,), 3),
+            (cq, (1,), 2),
+            (a2s, (0,), 0),
             (dp, (0,), 3),
             (ds, (1, 0), 3),
-            (bp, (0,), 1),
-            (bp, (2,), 1),
-            (cq, (1,), 2),
-            (bs, (1,), 1),
-            (bs, (3,), 1),
-            (bs, (0,), 1),
-            (a1, (0,), 0),
-            (a2p, (0,), 0),
-            (bs, (2,), 1),
-            (fv, (), 5),
-            (ds, (0, 1), 3),
-            (cg, (3,), 2),
             (cp, (0,), 1),
-            (cp, (1,), 1),
-            (cg, (0,), 5),
-            (ds, (1, 1), 3),
-            (e1, (0, 0), 4),
-            (cg, (2,), 4),
-            (e2, (0,), 4),
-            (ds, (0, 0), 3),
-            (cs, (0,), 2),
-            (dp, (2,), 3),
-            (e1, (1, 1), 4),
-            (cs, (1,), 2),
-            (cq, (3,), 2),
-            (cq, (2,), 2),
-            (cv, (0,), 1),
-            (a1, (1,), 0),
-            (a2s, (0,), 0),
-            (cs, (3,), 2),
             (a2p, (1,), 0),
-            (cs, (2,), 2),
-            (e1, (1, 0), 4),
-            (cp, (2,), 1),
-            (cv, (1,), 1),
-            (e2, (1,), 4),
-            (dp, (3,), 3),
-            (cq, (0,), 1),
+            (ds, (1, 1), 3),
+            (dp, (2,), 3),
+            (e2, (0,), 4),
+            (cp, (1,), 1),
+            (ds, (0, 0), 3),
+            (ca, (3,), 2),
+            (ds, (0, 1), 3),
+            (cv, (0,), 1),
             (a2s, (1,), 0),
+            (cgA, (0,), 2),
+            (e2, (1,), 4),
+            (cgP, (0,), 2),
+            (cgB, (0,), 2),
+            (cgM, (0,), 2),
             (ca, (0,), 1),
-            (ca, (1,), 1),
-            (cp, (3,), 1),
-            (ds, (2, 0), 3),
-            (cv, (2,), 1),
-            (ds, (3, 0), 3),
+            (cv, (1,), 1),
+            (dp, (3,), 3),
+            (fp, (), 4),
             (a3, (), 0),
             (ds, (2, 1), 3),
-            (cv, (3,), 1),
-            (ca, (2,), 1),
-            (fp, (), 4),
+            (ds, (2, 0), 3),
+            (ca, (1,), 1),
+            (ds, (3, 0), 3),
+            (cs, (1,), 2),
+            (fv, (), 4),
+            (st_out, (), 6),
+            (cq, (0,), 2),
+            (e1, (0, 1), 3),
+            (cs, (0,), 2),
+            (cp, (2,), 1),
+            (bp, (1,), 0),
         ]
         ctx.enter_context(tc.manual_schedule())
         a1(0, 0)
         a1(0, 1)
         weights()
-        for i in range(NCH + 5):
-            if i + 2 < NCH:
-                load(i + 2)
+        for i in range(NCH + 6):
             for fn, args, lag in steps:
                 c = i - lag
-                if 0 <= c < NCH and not (fn is a1 and c == 0):
-                    fn(c, *args)
+                if not 0 <= c < NCH or (fn is a1 and c == 0) or (fn is load and c <= 1):
+                    continue
+                fn(c, *args)
             if i == 0:
                 small_constants()
                 fc_weights()

@@ -6,11 +6,9 @@ from concourse.masks import make_identity
 B, H, H2, D_OUT = 8192, 512, 1024, 128
 P = 128
 T = 4
-J = 4
-CH = J * P
-NCH = B // CH
 EPS = 1e-5
 FLOPS = 2 * B * H * H + 2 * B * H2 * D_OUT
+SIZES = [2] + [4] * 15 + [2]
 
 F32 = mybir.dt.float32
 BF16 = mybir.dt.bfloat16
@@ -24,47 +22,30 @@ ALU = mybir.AluOpType
 
 def tile_rnnclassifier_pa_t_kernel(tc, h1_bytes, h1_scale, W_ih1, b_ih1, b_hh1, ln_g, ln_b, fc_W, fc_b, out):
     nc = tc.nc
-    x_view = h1_bytes.rearrange("(c q j) k -> c q j k", q=P, j=J)
-    out_view = out.rearrange("(c q j) f -> c q j f", q=P, j=J)
+    first = [sum(SIZES[:c]) * P for c in range(len(SIZES))]
+    nch = len(SIZES)
+
+    def rows(ap, c):
+        n = SIZES[c]
+        return ap[first[c] : first[c] + n * P, :].rearrange("(q j) k -> q j k", j=n)
 
     with ExitStack() as ctx:
         const = ctx.enter_context(tc.tile_pool(name="const", bufs=1))
-        loads = ctx.enter_context(tc.tile_pool(name="loads", bufs=3))
         work = ctx.enter_context(tc.tile_pool(name="work", bufs=2))
-        stat = ctx.enter_context(tc.tile_pool(name="stat", bufs=3))
-        ps_m = ctx.enter_context(tc.psum_pool(name="ps_m", bufs=1))
-        ps_s = ctx.enter_context(tc.psum_pool(name="ps_s", bufs=2))
-        ps_t = ctx.enter_context(tc.psum_pool(name="ps_t", bufs=1))
-        ps_q = ctx.enter_context(tc.psum_pool(name="ps_q", bufs=2))
-        ps_f = ctx.enter_context(tc.psum_pool(name="ps_f", bufs=2))
+        stat = ctx.enter_context(tc.tile_pool(name="stat", bufs=4))
+        ps_a = ctx.enter_context(tc.psum_pool(name="ps_a", bufs=2))
+        ps_s = ctx.enter_context(tc.psum_pool(name="ps_s", bufs=3))
+        ps_f = ctx.enter_context(tc.psum_pool(name="ps_f", bufs=3))
 
         xb, hx, xg, xc, xs = {}, {}, {}, {}, {}
-        hh, zz, mv, rs, nb = {}, {}, {}, {}, {}
+        hb, hh, zz, sm, nm, sq, rs, nb = {}, {}, {}, {}, {}, {}, {}, {}
+        mv = {}
         yy, yg, yc, ys = {}, {}, {}, {}
-        osb, tmb, tqb, fmb, xtb, s1b, ob, st = {}, {}, {}, {}, {}, {}, {}, {}
+        osb, fmb, xtb, s1b, ob = {}, {}, {}, {}, {}
 
         def load(c):
-            xb[c] = loads.tile([P, J, H], U8, name="x_bytes", align_bytes=64)
-            nc.sync.dma_start(out=xb[c][:], in_=x_view[c])
-
-        load(0)
-        scale = const.tile([P, 2, H], F32)
-        nc.sync.dma_start(out=scale[:, 0, :], in_=h1_scale.rearrange("o k -> (o k)").partition_broadcast(P))
-        w_sb = const.tile([P, T, H], BF16)
-        nc.sync.dma_start(out=w_sb[:], in_=W_ih1.rearrange("(m t) k -> m t k", t=T))
-        load(1)
-        f_sb = const.tile([P, H2], BF16)
-        nc.sync.dma_start(out=f_sb[:], in_=fc_W)
-        b1 = const.tile([P, T], BF16)
-        nc.gpsimd.dma_start(out=b1[:], in_=b_ih1.rearrange("(p t) -> p t", t=T))
-        b2 = const.tile([P, T], BF16)
-        nc.gpsimd.dma_start(out=b2[:], in_=b_hh1.rearrange("(p t) -> p t", t=T))
-        g_raw = const.tile([P, 2, T], BF16)
-        nc.gpsimd.dma_start(out=g_raw[:], in_=ln_g.rearrange("(o p t) -> p o t", o=2, t=T))
-        b_raw = const.tile([P, 2, T], BF16)
-        nc.gpsimd.dma_start(out=b_raw[:], in_=ln_b.rearrange("(o p t) -> p o t", o=2, t=T))
-        fcb_raw = const.tile([P, D_OUT], BF16)
-        nc.gpsimd.dma_start(out=fcb_raw[:], in_=fc_b.partition_broadcast(P))
+            xb[c] = work.tile([P, 4, H], U8, name="x_bytes", align_bytes=64, bufs=6)
+            nc.sync.dma_start(out=xb[c][:, : SIZES[c], :], in_=rows(h1_bytes, c))
 
         ident = const.tile([P, P], F32)
         make_identity(nc, ident[:])
@@ -72,13 +53,31 @@ def tile_rnnclassifier_pa_t_kernel(tc, h1_bytes, h1_scale, W_ih1, b_ih1, b_hh1, 
         nc.gpsimd.memset(half[:], -0.5)
         dummy = const.tile([P, 1], F32)
         nc.gpsimd.memset(dummy[:], 0.0)
-        nc.scalar.activation(out=dummy[:], in_=dummy[:], func=ACT.Tanh)
 
+        load(0)
+        scale = const.tile([P, 2, H], F32)
+        nc.sync.dma_start(out=scale[:, 0, :], in_=h1_scale.rearrange("o k -> (o k)").partition_broadcast(P))
+        w_sb = const.tile([P, T, H], BF16)
+        nc.sync.dma_start(out=w_sb[:], in_=W_ih1.rearrange("(m t) k -> m t k", t=T))
+        b1 = const.tile([P, H], BF16)
+        nc.scalar.dma_start(out=b1[:], in_=b_ih1.partition_broadcast(P))
+        b2 = const.tile([P, H], BF16)
+        nc.scalar.dma_start(out=b2[:], in_=b_hh1.partition_broadcast(P))
+        load(1)
+        f_sb = const.tile([P, H2], BF16)
+        nc.sync.dma_start(out=f_sb[:], in_=fc_W)
+        g_raw = const.tile([P, 2, T], BF16)
+        nc.gpsimd.dma_start(out=g_raw[:], in_=ln_g.rearrange("(o p t) -> p o t", o=2, t=T))
+        b_raw = const.tile([P, 2, T], BF16)
+        nc.gpsimd.dma_start(out=b_raw[:], in_=ln_b.rearrange("(o p t) -> p o t", o=2, t=T))
+        fcb_raw = const.tile([P, D_OUT], BF16)
+        nc.gpsimd.dma_start(out=fcb_raw[:], in_=fc_b.partition_broadcast(P))
+        nc.scalar.activation(out=dummy[:], in_=dummy[:], func=ACT.Tanh)
         nc.vector.tensor_copy(out=scale[:, 1, :], in_=scale[:, 0, :])
-        bsum = const.tile([P, T], F32)
+        bias = const.tile([P, H], F32)
         g_col = const.tile([P, 2, T], F32)
         b_col = const.tile([P, 2, T], F32)
-        fcb = const.tile([P, J, D_OUT], F32)
+        fcb = const.tile([P, 4, D_OUT], F32)
 
         w_grp = const.tile([P, H, T], BF16, align_bytes=64)
         w_codes = const.tile([P, H], U32, align_bytes=64)
@@ -90,143 +89,131 @@ def tile_rnnclassifier_pa_t_kernel(tc, h1_bytes, h1_scale, W_ih1, b_ih1, b_hh1, 
         def words(ap):
             return ap.bitcast(F32)
 
-        def turn(dst, block, as_matmul):
-            if as_matmul:
-                nc.tensor.matmul(dst, lhsT=block, rhs=ident[:], start=True, stop=True)
-            else:
-                nc.tensor.transpose(dst, block, ident[:])
-
         def a1(c, h):
-            if h == 0:
-                hx[c] = work.tile([P, J, H], BF16, name="hx", align_bytes=64, bufs=2)
-            dst = hx[c][:, 2 * h : 2 * h + 2, :].rearrange("p j k -> p (j k)")
-            code = xb[c][:, 2 * h : 2 * h + 2, :].rearrange("p j k -> p (j k)").bitcast(FP8)
-            nc.vector.tensor_tensor(out=dst, in0=code, in1=scale[:].rearrange("p a k -> p (a k)"), op=ALU.mult)
+            if c not in hx:
+                hx[c] = work.tile([P, 4, H], BF16, name="hx", align_bytes=64, bufs=3)
+            n = min(2, SIZES[c] - 2 * h)
+            dst = hx[c][:, 2 * h : 2 * h + n, :].rearrange("p j k -> p (j k)")
+            code = xb[c][:, 2 * h : 2 * h + n, :].rearrange("p j k -> p (j k)").bitcast(FP8)
+            nc.vector.tensor_tensor(out=dst, in0=code, in1=scale[:, :n, :].rearrange("p a k -> p (a k)"), op=ALU.mult)
 
         def a2p(c, h):
-            xtb[c, h] = ps_m.tile([P, 2, 2, P], F32, name="misc")
-            for jj in range(2):
+            n = min(2, SIZES[c] - 2 * h)
+            xtb[c, h] = ps_a.tile([P, 2, 2, P], F32, name="xt")
+            for jj in range(n):
                 w = words(hx[c][:, 2 * h + jj, :])
                 for u in range(2):
                     nc.tensor.transpose(xtb[c, h][:, jj, u, :], w[:, u : H // 2 : 2], ident[:])
 
         def a2s(c, h):
-            if h == 0:
-                xg[c] = work.tile([P, CH, T], BF16, name="xg", align_bytes=64, bufs=2)
-            dst = words(xg[c][:, h * 256 : h * 256 + 256, :]).rearrange("p (j r) u -> p j r u", j=2)
-            nc.scalar.copy(out=dst, in_=xtb[c, h][:].rearrange("p j u r -> p j r u"))
+            if c not in xg:
+                xg[c] = work.tile([P, 4 * P, T], BF16, name="xg", align_bytes=64, bufs=3)
+            n = min(2, SIZES[c] - 2 * h)
+            dst = words(xg[c][:, h * 256 : h * 256 + n * P, :]).rearrange("p (j r) u -> p j r u", j=n)
+            nc.scalar.copy(out=dst, in_=xtb[c, h][:, :n].rearrange("p j u r -> p j r u"))
 
         def a3(c):
-            xc[c] = work.tile([P, CH], U32, name="xc", align_bytes=64)
-            xs[c] = work.tile([P, CH], U8, name="xs", align_bytes=64)
-            nc.vector.quantize_mx(out=xc[c][:].bitcast(FP8X4), scales=xs[c][:], in_=xg[c][:].rearrange("p n t -> p (n t)"))
+            n = SIZES[c] * P
+            xc[c] = work.tile([P, 4 * P], U32, name="xc", align_bytes=64, bufs=4)
+            xs[c] = work.tile([P, 4 * P], U8, name="xs", align_bytes=64, bufs=4)
+            nc.vector.quantize_mx(out=xc[c][:, :n].bitcast(FP8X4), scales=xs[c][:, :n], in_=xg[c][:, :n, :].rearrange("p n t -> p (n t)"))
 
-        def bp(c, t):
-            s1b[c, t] = ps_s.tile([P, CH], F32, name="s1")
+        def bp(c, j):
+            s1b[c, j] = ps_s.tile([P, H], F32, name="s1")
             nc.tensor.matmul_mx(
-                out=s1b[c, t][:],
-                lhsT=w_codes[:, t * P : (t + 1) * P].bitcast(FP8X4),
-                lhsT_scale=w_scales[:, t * P : (t + 1) * P],
-                rhs=xc[c][:].bitcast(FP8X4),
-                rhs_scale=xs[c][:],
+                out=s1b[c, j][:],
+                lhsT=xc[c][:, j * P : (j + 1) * P].bitcast(FP8X4),
+                lhsT_scale=xs[c][:, j * P : (j + 1) * P],
+                rhs=w_codes[:].bitcast(FP8X4),
+                rhs_scale=w_scales[:],
                 start=True,
                 stop=True,
             )
 
-        def bs(c, t):
-            if c not in hh:
-                hh[c] = work.tile([P, T, CH], F32, name="hh", bufs=3)
-            nc.scalar.activation(out=hh[c][:, t, :], in_=s1b[c, t][:], func=ACT.Tanh, bias=bsum[:, t : t + 1])
+        def bv(c, j):
+            hb[c, j] = work.tile([P, H], F32, name="hb", bufs=4)
+            nc.vector.tensor_tensor(out=hb[c, j][:], in0=s1b[c, j][:], in1=bias[:], op=ALU.add)
 
-        def cp(c, j):
-            tmb[c, j] = ps_t.tile([P, T, P], F32, name="tm")
-            for t in range(T):
-                turn(tmb[c, j][:, t, :], hh[c][:, t, j * P : (j + 1) * P], t == 0)
+        def bs(c, j):
+            if c not in hh:
+                hh[c] = work.tile([P, 4, H], F32, name="hh", bufs=3)
+                sm[c] = stat.tile([P, 4], F32, name="sm")
+                nm[c] = stat.tile([P, 4], F32, name="nm")
+                sq[c] = stat.tile([P, 4], F32, name="sq")
+                rs[c] = stat.tile([P, 4], F32, name="rs")
+                nb[c] = stat.tile([P, 4], F32, name="nb")
+            nc.scalar.activation(out=hh[c][:, j, :], in_=hb[c, j][:], func=ACT.Tanh, accum_out=sm[c][:, j : j + 1])
+
+        def cgN(c):
+            n = SIZES[c]
+            nc.gpsimd.tensor_scalar(out=nm[c][:, :n], in0=sm[c][:, :n], scalar1=-1.0 / H, scalar2=0.0, op0=ALU.mult, op1=ALU.add)
 
         def cq(c, j):
-            tqb[c, j] = ps_q.tile([P, T, P], F32, name="tq")
-            for t in range(T):
-                nc.tensor.transpose(tqb[c, j][:, t, :], hh[c][:, t, j * P : (j + 1) * P], ident[:])
+            junk = work.tile([P, H], BF16, name="junk", bufs=2)
+            nc.scalar.activation(out=junk[:], in_=hh[c][:, j, :], func=ACT.Square, bias=nm[c][:, j : j + 1], accum_out=sq[c][:, j : j + 1])
 
-        def cv(c, j):
-            if c not in mv:
-                mv[c] = stat.tile([P, J, 2], F32, name="mv")
-                rs[c] = stat.tile([P, J], F32, name="rs")
-                nb[c] = stat.tile([P, J], F32, name="nb")
-                st[c] = stat.tile([P, J, 6], F32, name="st")
-            nc.vector.bn_stats(out=st[c][:, j, :], in_=tmb[c, j][:].rearrange("p t m -> p (t m)"))
+        def cgA(c):
+            n = SIZES[c]
+            nc.gpsimd.tensor_scalar(out=rs[c][:, :n], in0=sq[c][:, :n], scalar1=1.0 / H, scalar2=EPS, op0=ALU.mult, op1=ALU.add)
 
-        def ca(c, j):
-            nc.vector.bn_aggr(out=mv[c][:, j, :], in_=st[c][:, j, :])
+        def cgP(c):
+            n = SIZES[c]
+            nc.gpsimd.tensor_tensor(out=rs[c][:, :n], in0=rs[c][:, :n], in1=half[:, :n], op=ALU.pow)
 
-        def cgA(c, q):
-            js = slice(4 * q, 4 * q + 4)
-            nc.gpsimd.tensor_scalar(out=rs[c][:, js], in0=mv[c][:, js, 1], scalar1=EPS, scalar2=None, op0=ALU.add)
-
-        def cgB(c, q):
-            js = slice(4 * q, 4 * q + 4)
-            nc.gpsimd.tensor_scalar(out=nb[c][:, js], in0=mv[c][:, js, 0], scalar1=-1.0, scalar2=None, op0=ALU.mult)
-
-        def cgP(c, q):
-            js = slice(4 * q, 4 * q + 4)
-            nc.gpsimd.tensor_tensor(out=rs[c][:, js], in0=rs[c][:, js], in1=half[:], op=ALU.pow)
-
-        def cgM(c, q):
-            js = slice(4 * q, 4 * q + 4)
-            nc.gpsimd.tensor_tensor(out=nb[c][:, js], in0=nb[c][:, js], in1=rs[c][:, js], op=ALU.mult)
+        def cgM(c):
+            n = SIZES[c]
+            nc.gpsimd.tensor_tensor(out=nb[c][:, :n], in0=nm[c][:, :n], in1=rs[c][:, :n], op=ALU.mult)
 
         def cs(c, j):
             if c not in zz:
-                zz[c] = work.tile([P, J, H], F32, name="zz", bufs=2)
-            src = tqb[c, j][:].rearrange("p t m -> p (t m)")
-            if j in []:
-                nc.vector.tensor_scalar(
-                    out=zz[c][:, j, :], in0=src, scalar1=rs[c][:, j : j + 1], scalar2=nb[c][:, j : j + 1], op0=ALU.mult, op1=ALU.add
-                )
-            else:
-                nc.scalar.activation(out=zz[c][:, j, :], in_=src, func=ACT.Identity, scale=rs[c][:, j : j + 1], bias=nb[c][:, j : j + 1])
+                zz[c] = work.tile([P, 4, H], F32, name="zz", bufs=3)
+            eng = nc.vector
+            eng.tensor_scalar(
+                out=zz[c][:, j, :], in0=hh[c][:, j, :], scalar1=rs[c][:, j : j + 1], scalar2=nb[c][:, j : j + 1], op0=ALU.mult, op1=ALU.add
+            )
 
         def dp(c, t):
-            fmb[c, t] = ps_f.tile([P, CH], F32, name="fm")
-            for j in range(J):
-                turn(fmb[c, t][:, j * P : (j + 1) * P], zz[c][:, j, t * P : (t + 1) * P], j == 0)
+            fmb[c, t] = ps_f.tile([P, 4 * P], F32, name="fm")
+            for j in range(SIZES[c]):
+                nc.tensor.transpose(fmb[c, t][:, j * P : (j + 1) * P], zz[c][:, j, t * P : (t + 1) * P], ident[:])
+
+        on_vector_last = []
+        on_vector_odd = []
+        on_vector_all = []
 
         def ds(c, t, o):
+            n = SIZES[c] * P
             if (c, o) not in yy:
-                yy[c, o] = work.tile([P, T, CH], BF16, name="yy%d" % o, bufs=2)
-            if 2 * t + o in []:
-                nc.vector.tensor_scalar(
-                    out=yy[c, o][:, t, :], in0=fmb[c, t][:], scalar1=g_col[:, o, t : t + 1], scalar2=b_col[:, o, t : t + 1], op0=ALU.mult, op1=ALU.add
-                )
+                yy[c, o] = work.tile([P, T, 4 * P], BF16, name="yy%d" % o, bufs=3)
+            dst, src = yy[c, o][:, t, :n], fmb[c, t][:, :n]
+            scl, sft = g_col[:, o, t : t + 1], b_col[:, o, t : t + 1]
+            if (c == nch - 1 and (t, o) in on_vector_last) or (c < nch - 1 and c % 2 == 1 and (t, o) in on_vector_odd) or (c % 2 == 0 and c < nch - 1 and (t, o) in on_vector_all):
+                nc.vector.tensor_scalar(out=dst, in0=src, scalar1=scl, scalar2=sft, op0=ALU.mult, op1=ALU.add)
             else:
-                nc.scalar.activation(
-                    out=yy[c, o][:, t, :], in_=fmb[c, t][:], func=ACT.Identity, scale=g_col[:, o, t : t + 1], bias=b_col[:, o, t : t + 1]
-                )
+                nc.scalar.activation(out=dst, in_=src, func=ACT.Identity, scale=scl, bias=sft)
+
+        parts = [[4],[4]]
 
         def e1(c, o, part):
             if (c, o) not in yg:
-                yg[c, o] = work.tile([P, CH, T], BF16, name="yg%d" % o, align_bytes=64, bufs=2)
-            if 2 * o + part in []:
-                for q in range(2):
-                    ns = slice(256 * part + 128 * q, 256 * part + 128 * q + 128)
-                    nc.gpsimd.tensor_scalar(
-                        out=yg[c, o][:, ns, :], in0=yy[c, o][:, :, ns].rearrange("p t n -> p n t"), scalar1=1.0, scalar2=0.0, op0=ALU.mult, op1=ALU.add
-                    )
-            else:
-                ns = slice(256 * part, 256 * part + 256)
-                nc.vector.tensor_copy(
-                    out=yg[c, o][:, ns, :].rearrange("p (n i) t -> p n t i", i=4),
-                    in_=yy[c, o][:, :, ns].rearrange("p t (n i) -> p n t i", i=4),
-                )
+                yg[c, o] = work.tile([P, 4 * P, T], BF16, name="yg%d" % o, align_bytes=64, bufs=3)
+            a = sum(parts[o][:part]) * 32 * SIZES[c]
+            ns = slice(a, a + parts[o][part] * 32 * SIZES[c])
+            nc.vector.tensor_copy(
+                out=yg[c, o][:, ns, :].rearrange("p (n i) t -> p n t i", i=4),
+                in_=yy[c, o][:, :, ns].rearrange("p t (n i) -> p n t i", i=4),
+            )
 
         def e2(c, o):
-            yc[c, o] = work.tile([P, CH], U32, name="yc%d" % o, align_bytes=64)
-            ys[c, o] = work.tile([P, CH], U8, name="ys%d" % o, align_bytes=64)
-            nc.vector.quantize_mx(out=yc[c, o][:].bitcast(FP8X4), scales=ys[c, o][:], in_=yg[c, o][:].rearrange("p n t -> p (n t)"))
+            n = SIZES[c] * P
+            yc[c, o] = work.tile([P, 4 * P], U32, name="yc%d" % o, align_bytes=64, bufs=3)
+            ys[c, o] = work.tile([P, 4 * P], U8, name="ys%d" % o, align_bytes=64, bufs=3)
+            nc.vector.quantize_mx(out=yc[c, o][:, :n].bitcast(FP8X4), scales=ys[c, o][:, :n], in_=yg[c, o][:, :n, :].rearrange("p n t -> p (n t)"))
 
         def fp(c):
-            ob[c] = ps_m.tile([P, J, D_OUT], F32, name="misc")
-            for j in range(J):
+            xo = ps_a.tile([P, 2, 2, P], F32, name="xt")
+            ob[c] = xo[:].rearrange("p a b r -> p (a b) r")
+            for j in range(SIZES[c]):
                 for o in range(2):
                     nc.tensor.matmul_mx(
                         out=ob[c][:, j, :],
@@ -239,113 +226,108 @@ def tile_rnnclassifier_pa_t_kernel(tc, h1_bytes, h1_scale, W_ih1, b_ih1, b_hh1, 
                     )
 
         def fv(c):
-            osb[c] = work.tile([P, J, D_OUT], F32, name="osb")
-            nc.vector.tensor_tensor(out=osb[c][:], in0=ob[c][:], in1=fcb[:], op=ALU.add)
+            n = SIZES[c]
+            osb[c] = work.tile([P, 4, D_OUT], F32, name="osb", bufs=3)
+            nc.vector.tensor_tensor(out=osb[c][:, :n, :], in0=ob[c][:, :n, :], in1=fcb[:, :n, :], op=ALU.add)
 
         def st_out(c):
-            nc.sync.dma_start(out=out_view[c], in_=osb[c][:])
+            nc.sync.dma_start(out=rows(out, c), in_=osb[c][:, : SIZES[c], :])
+
+        def turn_weights(src, pieces, grp):
+            xt = ps_f.tile([P, 4 * P], F32, name="fm")
+            v = xt[:].rearrange("p (a u r) -> p a u r", a=2, u=2)
+            for a in range(2):
+                for u in range(2):
+                    nc.tensor.transpose(v[:, a, u, :], pieces[a][:, u : H // 2 : 2], ident[:])
+            nc.scalar.copy(out=words(grp).rearrange("p (j r) u -> p j r u", j=2), in_=v.rearrange("p j u r -> p j r u"))
 
         def weights():
             for h in range(2):
-                xt = ps_m.tile([P, 2, 2, P], F32, name="misc")
-                for tt in range(2):
-                    w = words(w_sb[:, 2 * h + tt, :])
-                    for u in range(2):
-                        nc.tensor.transpose(xt[:, tt, u, :], w[:, u : H // 2 : 2], ident[:])
-                dst = words(w_grp[:, h * 256 : h * 256 + 256, :]).rearrange("p (j r) u -> p j r u", j=2)
-                nc.scalar.copy(out=dst, in_=xt[:].rearrange("p j u r -> p j r u"))
+                turn_weights(None, [words(w_sb[:, 2 * h + a, :]) for a in range(2)], w_grp[:, h * 256 : h * 256 + 256, :])
             nc.vector.quantize_mx(out=w_codes[:].bitcast(FP8X4), scales=w_scales[:], in_=w_grp[:].rearrange("p n t -> p (n t)"))
 
-        def fc_weights():
-            xt = ps_m.tile([P, 2, 2, P], F32, name="misc")
-            w = words(f_sb[:])
-            for o in range(2):
-                for u in range(2):
-                    nc.tensor.transpose(xt[:, o, u, :], w[:, 256 * o + u : 256 * (o + 1) : 2], ident[:])
-            dst = words(f_grp[:]).rearrange("p (j r) u -> p j r u", j=2)
-            nc.scalar.copy(out=dst, in_=xt[:].rearrange("p j u r -> p j r u"))
-            nc.vector.quantize_mx(out=f_codes[:].bitcast(FP8X4), scales=f_scales[:], in_=f_grp[:].rearrange("p n t -> p (n t)"))
-
         def small_constants():
-            nc.vector.tensor_tensor(out=bsum[:], in0=b1[:], in1=b2[:], op=ALU.add)
+            nc.vector.tensor_tensor(
+                out=bias[:].rearrange("p (t m) -> p t m", t=T),
+                in0=b1[:].rearrange("p (m t) -> p t m", t=T),
+                in1=b2[:].rearrange("p (m t) -> p t m", t=T),
+                op=ALU.add,
+            )
+
+        def late_constants():
             nc.vector.tensor_copy(out=g_col[:], in_=g_raw[:])
             nc.vector.tensor_copy(out=b_col[:], in_=b_raw[:])
-            for j in range(J):
+            for j in range(4):
                 nc.vector.tensor_copy(out=fcb[:, j, :], in_=fcb_raw[:])
+            fw = words(f_sb[:])
+            turn_weights(None, [fw[:, 256 * o : 256 * (o + 1)] for o in range(2)], f_grp[:])
+            nc.vector.quantize_mx(out=f_codes[:].bitcast(FP8X4), scales=f_scales[:], in_=f_grp[:].rearrange("p n t -> p (n t)"))
 
         steps = [
-            (cv, (2,), 2),
-            (bs, (1,), 1),
-            (bp, (2,), 1),
-            (cq, (2,), 3),
-            (e1, (0, 0), 4),
-            (cq, (3,), 3),
-            (cp, (3,), 2),
+            (bp, (2,), 2),
+            (bv, (1,), 2),
+            (bp, (0,), 2),
+            (cs, (0,), 4),
+            (cs, (1,), 4),
             (load, (), 0),
-            (a1, (0,), 0),
-            (bs, (2,), 1),
-            (ca, (2,), 2),
-            (cv, (3,), 2),
+            (dp, (2,), 4),
             (a1, (1,), 0),
-            (cs, (2,), 3),
-            (bp, (3,), 1),
-            (cs, (3,), 3),
-            (ds, (3, 1), 4),
-            (bs, (3,), 1),
-            (bp, (0,), 1),
-            (e1, (1, 0), 4),
-            (bs, (0,), 1),
-            (a2p, (0,), 0),
-            (e1, (1, 1), 4),
-            (dp, (1,), 3),
-            (cq, (1,), 2),
-            (a2s, (0,), 0),
-            (dp, (0,), 3),
-            (ds, (1, 0), 3),
-            (cp, (0,), 1),
+            (cgN, (), 3),
+            (dp, (3,), 4),
+            (a2p, (0,), 1),
+            (cq, (2,), 3),
+            (cq, (3,), 3),
+            (bv, (2,), 2),
+            (e1, (0, 0), 5),
+            (cq, (1,), 3),
+            (cq, (0,), 3),
+            (fp, (), 6),
+            (ds, (2, 0), 4),
+            (e1, (1, 0), 5),
+            (bs, (1,), 2),
+            (e2, (0,), 5),
+            (cgA, (), 3),
+            (bp, (3,), 2),
+            (a2s, (0,), 1),
+            (bv, (0,), 2),
+            (cgP, (), 3),
+            (bv, (3,), 2),
+            (fv, (), 6),
+            (bs, (2,), 2),
+            (dp, (0,), 4),
+            (ds, (2, 1), 4),
+            (cgM, (), 3),
+            (ds, (3, 0), 4),
             (a2p, (1,), 0),
-            (ds, (1, 1), 3),
-            (dp, (2,), 3),
-            (e2, (0,), 4),
-            (cp, (1,), 1),
-            (ds, (0, 0), 3),
-            (ca, (3,), 2),
-            (ds, (0, 1), 3),
-            (cv, (0,), 1),
-            (a2s, (1,), 0),
-            (cgA, (0,), 2),
-            (e2, (1,), 4),
-            (cgP, (0,), 2),
-            (cgB, (0,), 2),
-            (cgM, (0,), 2),
-            (ca, (0,), 1),
-            (cv, (1,), 1),
-            (dp, (3,), 3),
-            (fp, (), 4),
-            (a3, (), 0),
-            (ds, (2, 1), 3),
-            (ds, (2, 0), 3),
-            (ca, (1,), 1),
-            (ds, (3, 0), 3),
-            (cs, (1,), 2),
-            (fv, (), 4),
+            (ds, (0, 0), 4),
+            (dp, (1,), 4),
             (st_out, (), 6),
-            (cq, (0,), 2),
-            (e1, (0, 1), 3),
-            (cs, (0,), 2),
-            (cp, (2,), 1),
-            (bp, (1,), 0),
+            (bs, (0,), 2),
+            (bs, (3,), 2),
+            (a3, (), 1),
+            (e2, (1,), 5),
+            (cs, (2,), 3),
+            (ds, (1, 0), 4),
+            (ds, (3, 1), 4),
+            (a2s, (1,), 0),
+            (ds, (0, 1), 4),
+            (bp, (1,), 1),
+            (a1, (0,), 0),
+            (cs, (3,), 3),
+            (ds, (1, 1), 4),
         ]
         ctx.enter_context(tc.manual_schedule())
-        a1(0, 0)
-        a1(0, 1)
+        for h in range((SIZES[0] + 1) // 2):
+            a1(0, h)
         weights()
-        for i in range(NCH + 6):
+        small_constants()
+        for i in range(nch + 7):
             for fn, args, lag in steps:
                 c = i - lag
-                if not 0 <= c < NCH or (fn is a1 and c == 0) or (fn is load and c <= 1):
+                if not 0 <= c < nch or (fn is a1 and c == 0) or (fn is load and c <= 1):
+                    continue
+                if fn in (a1, a2p, a2s) and 2 * args[0] >= SIZES[c] or fn in (bp, bv, bs, cq, cs) and args[0] >= SIZES[c]:
                     continue
                 fn(c, *args)
-            if i == 0:
-                small_constants()
-                fc_weights()
+            if i == 1:
+                late_constants()

@@ -47,6 +47,12 @@ def tile_rnnclassifier_pa_t_kernel(tc, h1_bytes, h1_scale, W_ih1, b_ih1, b_hh1, 
             xb[c] = work.tile([P, 4, H], U8, name="x_bytes", align_bytes=64, bufs=6)
             nc.sync.dma_start(out=xb[c][:, : SIZES[c], :], in_=rows(h1_bytes, c))
 
+        row_b = const.tile([P, H], BF16)
+        nc.vector.memset(row_b[:], 0.0)
+        row_f = const.tile([P, D_OUT], BF16)
+        nc.vector.memset(row_f[:], 0.0)
+        ones = const.tile([P, P], BF16)
+        nc.vector.memset(ones[:], 1.0)
         ident = const.tile([P, P], F32)
         make_identity(nc, ident[:])
         half = const.tile([P, 4], F32)
@@ -59,10 +65,8 @@ def tile_rnnclassifier_pa_t_kernel(tc, h1_bytes, h1_scale, W_ih1, b_ih1, b_hh1, 
         nc.sync.dma_start(out=scale[:, 0, :], in_=h1_scale.rearrange("o k -> (o k)").partition_broadcast(P))
         w_sb = const.tile([P, T, H], BF16)
         nc.sync.dma_start(out=w_sb[:], in_=W_ih1.rearrange("(m t) k -> m t k", t=T))
-        b1 = const.tile([P, H], BF16)
-        nc.scalar.dma_start(out=b1[:], in_=b_ih1.partition_broadcast(P))
-        b2 = const.tile([P, H], BF16)
-        nc.scalar.dma_start(out=b2[:], in_=b_hh1.partition_broadcast(P))
+        nc.scalar.dma_start(out=row_b[0:1, :], in_=b_ih1.rearrange("(o k) -> o k", o=1))
+        nc.scalar.dma_start(out=row_b[1:2, :], in_=b_hh1.rearrange("(o k) -> o k", o=1))
         load(1)
         f_sb = const.tile([P, H2], BF16)
         nc.sync.dma_start(out=f_sb[:], in_=fc_W)
@@ -70,10 +74,9 @@ def tile_rnnclassifier_pa_t_kernel(tc, h1_bytes, h1_scale, W_ih1, b_ih1, b_hh1, 
         nc.gpsimd.dma_start(out=g_raw[:], in_=ln_g.rearrange("(o p t) -> p o t", o=2, t=T))
         b_raw = const.tile([P, 2, T], BF16)
         nc.gpsimd.dma_start(out=b_raw[:], in_=ln_b.rearrange("(o p t) -> p o t", o=2, t=T))
-        fcb_raw = const.tile([P, D_OUT], BF16)
-        nc.gpsimd.dma_start(out=fcb_raw[:], in_=fc_b.partition_broadcast(P))
+        nc.gpsimd.dma_start(out=row_f[0:1, :], in_=fc_b.rearrange("(o k) -> o k", o=1))
         nc.scalar.activation(out=dummy[:], in_=dummy[:], func=ACT.Tanh)
-        nc.vector.tensor_copy(out=scale[:, 1, :], in_=scale[:, 0, :])
+        nc.scalar.copy(out=scale[:, 1, :], in_=scale[:, 0, :])
         bias = const.tile([P, H], F32)
         g_col = const.tile([P, 2, T], F32)
         b_col = const.tile([P, 2, T], F32)
@@ -95,6 +98,10 @@ def tile_rnnclassifier_pa_t_kernel(tc, h1_bytes, h1_scale, W_ih1, b_ih1, b_hh1, 
             n = min(2, SIZES[c] - 2 * h)
             dst = hx[c][:, 2 * h : 2 * h + n, :].rearrange("p j k -> p (j k)")
             code = xb[c][:, 2 * h : 2 * h + n, :].rearrange("p j k -> p (j k)").bitcast(FP8)
+            if c == 0:
+                for j in range(2 * h, 2 * h + n):
+                    nc.vector.tensor_tensor(out=hx[c][:, j, :], in0=xb[c][:, j, :].bitcast(FP8), in1=scale[:, 0, :], op=ALU.mult)
+                return
             nc.vector.tensor_tensor(out=dst, in0=code, in1=scale[:, :n, :].rearrange("p a k -> p (a k)"), op=ALU.mult)
 
         def a2p(c, h):
@@ -141,7 +148,6 @@ def tile_rnnclassifier_pa_t_kernel(tc, h1_bytes, h1_scale, W_ih1, b_ih1, b_hh1, 
                 nm[c] = stat.tile([P, 4], F32, name="nm")
                 sq[c] = stat.tile([P, 4], F32, name="sq")
                 rs[c] = stat.tile([P, 4], F32, name="rs")
-                nb[c] = stat.tile([P, 4], F32, name="nb")
             nc.scalar.activation(out=hh[c][:, j, :], in_=hb[c, j][:], func=ACT.Tanh, accum_out=sm[c][:, j : j + 1])
 
         def cgN(c):
@@ -150,26 +156,22 @@ def tile_rnnclassifier_pa_t_kernel(tc, h1_bytes, h1_scale, W_ih1, b_ih1, b_hh1, 
 
         def cq(c, j):
             junk = work.tile([P, H], BF16, name="junk", bufs=2)
-            nc.scalar.activation(out=junk[:], in_=hh[c][:, j, :], func=ACT.Square, bias=nm[c][:, j : j + 1], accum_out=sq[c][:, j : j + 1])
+            nc.scalar.activation(out=junk[:], in_=hh[c][:, j, :], func=ACT.Square, scale=-float(H), bias=sm[c][:, j : j + 1], accum_out=sq[c][:, j : j + 1])
 
         def cgA(c):
             n = SIZES[c]
-            nc.gpsimd.tensor_scalar(out=rs[c][:, :n], in0=sq[c][:, :n], scalar1=1.0 / H, scalar2=EPS, op0=ALU.mult, op1=ALU.add)
+            nc.gpsimd.tensor_scalar(out=rs[c][:, :n], in0=sq[c][:, :n], scalar1=1.0 / H**3, scalar2=EPS, op0=ALU.mult, op1=ALU.add)
 
         def cgP(c):
             n = SIZES[c]
             nc.gpsimd.tensor_tensor(out=rs[c][:, :n], in0=rs[c][:, :n], in1=half[:, :n], op=ALU.pow)
 
-        def cgM(c):
-            n = SIZES[c]
-            nc.gpsimd.tensor_tensor(out=nb[c][:, :n], in0=nm[c][:, :n], in1=rs[c][:, :n], op=ALU.mult)
-
         def cs(c, j):
             if c not in zz:
                 zz[c] = work.tile([P, 4, H], F32, name="zz", bufs=3)
-            eng = nc.vector
+            eng = nc.gpsimd if "GVGV"[j] == "G" else nc.vector
             eng.tensor_scalar(
-                out=zz[c][:, j, :], in0=hh[c][:, j, :], scalar1=rs[c][:, j : j + 1], scalar2=nb[c][:, j : j + 1], op0=ALU.mult, op1=ALU.add
+                out=zz[c][:, j, :], in0=hh[c][:, j, :], scalar1=nm[c][:, j : j + 1], scalar2=rs[c][:, j : j + 1], op0=ALU.add, op1=ALU.mult
             )
 
         def dp(c, t):
@@ -177,9 +179,7 @@ def tile_rnnclassifier_pa_t_kernel(tc, h1_bytes, h1_scale, W_ih1, b_ih1, b_hh1, 
             for j in range(SIZES[c]):
                 nc.tensor.transpose(fmb[c, t][:, j * P : (j + 1) * P], zz[c][:, j, t * P : (t + 1) * P], ident[:])
 
-        on_vector_last = []
-        on_vector_odd = []
-        on_vector_all = []
+        affine_on_vector = {"even": [], "odd": [(3, 1)], "last": []}
 
         def ds(c, t, o):
             n = SIZES[c] * P
@@ -187,7 +187,7 @@ def tile_rnnclassifier_pa_t_kernel(tc, h1_bytes, h1_scale, W_ih1, b_ih1, b_hh1, 
                 yy[c, o] = work.tile([P, T, 4 * P], BF16, name="yy%d" % o, bufs=3)
             dst, src = yy[c, o][:, t, :n], fmb[c, t][:, :n]
             scl, sft = g_col[:, o, t : t + 1], b_col[:, o, t : t + 1]
-            if (c == nch - 1 and (t, o) in on_vector_last) or (c < nch - 1 and c % 2 == 1 and (t, o) in on_vector_odd) or (c % 2 == 0 and c < nch - 1 and (t, o) in on_vector_all):
+            if (t, o) in affine_on_vector["last" if c == nch - 1 else ("odd" if c % 2 else "even")]:
                 nc.vector.tensor_scalar(out=dst, in0=src, scalar1=scl, scalar2=sft, op0=ALU.mult, op1=ALU.add)
             else:
                 nc.scalar.activation(out=dst, in_=src, func=ACT.Identity, scale=scl, bias=sft)
@@ -244,87 +244,91 @@ def tile_rnnclassifier_pa_t_kernel(tc, h1_bytes, h1_scale, W_ih1, b_ih1, b_hh1, 
         def weights():
             for h in range(2):
                 turn_weights(None, [words(w_sb[:, 2 * h + a, :]) for a in range(2)], w_grp[:, h * 256 : h * 256 + 256, :])
+        def weights_quantised():
             nc.vector.quantize_mx(out=w_codes[:].bitcast(FP8X4), scales=w_scales[:], in_=w_grp[:].rearrange("p n t -> p (n t)"))
 
         def small_constants():
-            nc.vector.tensor_tensor(
-                out=bias[:].rearrange("p (t m) -> p t m", t=T),
-                in0=b1[:].rearrange("p (m t) -> p t m", t=T),
-                in1=b2[:].rearrange("p (m t) -> p t m", t=T),
-                op=ALU.add,
-            )
+            bk = ps_f.tile([P, 4 * P], F32, name="fm")
+            nc.tensor.matmul(bk[:], lhsT=ones[:], rhs=row_b[:], start=True, stop=True)
+            nc.scalar.copy(out=bias[:].rearrange("p (t m) -> p t m", t=T), in_=bk[:].rearrange("p (m t) -> p t m", t=T))
 
         def late_constants():
-            nc.vector.tensor_copy(out=g_col[:], in_=g_raw[:])
-            nc.vector.tensor_copy(out=b_col[:], in_=b_raw[:])
+            nc.gpsimd.tensor_copy(out=g_col[:], in_=g_raw[:])
+            nc.gpsimd.tensor_copy(out=b_col[:], in_=b_raw[:])
+            fk = ps_f.tile([P, 4 * P], F32, name="fm")
             for j in range(4):
-                nc.vector.tensor_copy(out=fcb[:, j, :], in_=fcb_raw[:])
+                nc.tensor.matmul(fk[:, j * P : (j + 1) * P], lhsT=ones[:], rhs=row_f[:], start=True, stop=True)
+            nc.scalar.copy(out=fcb[:].rearrange("p j f -> p (j f)"), in_=fk[:])
             fw = words(f_sb[:])
             turn_weights(None, [fw[:, 256 * o : 256 * (o + 1)] for o in range(2)], f_grp[:])
             nc.vector.quantize_mx(out=f_codes[:].bitcast(FP8X4), scales=f_scales[:], in_=f_grp[:].rearrange("p n t -> p (n t)"))
 
         steps = [
-            (bp, (2,), 2),
-            (bv, (1,), 2),
-            (bp, (0,), 2),
-            (cs, (0,), 4),
-            (cs, (1,), 4),
+            (e2, (0,), 6),
+            (dp, (3,), 5),
+            (cgP, (), 4),
+            (a2p, (1,), 1),
             (load, (), 0),
-            (dp, (2,), 4),
-            (a1, (1,), 0),
-            (cgN, (), 3),
-            (dp, (3,), 4),
-            (a2p, (0,), 1),
-            (cq, (2,), 3),
-            (cq, (3,), 3),
-            (bv, (2,), 2),
-            (e1, (0, 0), 5),
-            (cq, (1,), 3),
-            (cq, (0,), 3),
-            (fp, (), 6),
-            (ds, (2, 0), 4),
-            (e1, (1, 0), 5),
-            (bs, (1,), 2),
-            (e2, (0,), 5),
-            (cgA, (), 3),
-            (bp, (3,), 2),
+            (bp, (2,), 3),
+            (ds, (2, 1), 5),
             (a2s, (0,), 1),
-            (bv, (0,), 2),
-            (cgP, (), 3),
-            (bv, (3,), 2),
-            (fv, (), 6),
-            (bs, (2,), 2),
-            (dp, (0,), 4),
-            (ds, (2, 1), 4),
-            (cgM, (), 3),
-            (ds, (3, 0), 4),
-            (a2p, (1,), 0),
-            (ds, (0, 0), 4),
-            (dp, (1,), 4),
-            (st_out, (), 6),
-            (bs, (0,), 2),
-            (bs, (3,), 2),
-            (a3, (), 1),
-            (e2, (1,), 5),
-            (cs, (2,), 3),
-            (ds, (1, 0), 4),
-            (ds, (3, 1), 4),
-            (a2s, (1,), 0),
-            (ds, (0, 1), 4),
-            (bp, (1,), 1),
+            (ds, (1, 1), 5),
+            (ds, (2, 0), 5),
+            (bv, (3,), 3),
+            (cs, (2,), 4),
+            (ds, (3, 1), 5),
+            (ds, (1, 0), 5),
+            (bv, (2,), 3),
+            (bp, (0,), 2),
+            (bs, (0,), 3),
+            (ds, (3, 0), 5),
+            (a2s, (1,), 1),
+            (bs, (1,), 3),
+            (cs, (1,), 4),
             (a1, (0,), 0),
-            (cs, (3,), 3),
-            (ds, (1, 1), 4),
+            (bp, (3,), 2),
+            (cq, (0,), 3),
+            (cs, (3,), 4),
+            (bs, (3,), 3),
+            (cq, (1,), 3),
+            (cs, (0,), 4),
+            (e1, (1, 0), 5),
+            (e1, (0, 0), 5),
+            (a1, (1,), 0),
+            (dp, (0,), 4),
+            (fp, (), 6),
+            (bs, (2,), 3),
+            (dp, (2,), 4),
+            (a2p, (0,), 0),
+            (e2, (1,), 5),
+            (bv, (0,), 2),
+            (cq, (3,), 3),
+            (cq, (2,), 3),
+            (ds, (0, 1), 4),
+            (a3, (), 1),
+            (bp, (1,), 2),
+            (fv, (), 6),
+            (bv, (1,), 2),
+            (ds, (0, 0), 4),
+            (st_out, (), 6),
+            (dp, (1,), 4),
+            (cgN, (), 3),
+            (cgA, (), 3),
         ]
         ctx.enter_context(tc.manual_schedule())
-        for h in range((SIZES[0] + 1) // 2):
-            a1(0, h)
+        a1(0, 0)
+        a2p(0, 0)
+        a2s(0, 0)
+        a1(1, 0)
+        a3(0)
         weights()
+        weights_quantised()
         small_constants()
+        early = [(a1, 0, 0), (a2p, 0, 0), (a2s, 0, 0), (a3, 0), (a1, 1, 0)]
         for i in range(nch + 7):
             for fn, args, lag in steps:
                 c = i - lag
-                if not 0 <= c < nch or (fn is a1 and c == 0) or (fn is load and c <= 1):
+                if not 0 <= c < nch or (fn, c, *args) in early or (fn is load and c <= 1):
                     continue
                 if fn in (a1, a2p, a2s) and 2 * args[0] >= SIZES[c] or fn in (bp, bv, bs, cq, cs) and args[0] >= SIZES[c]:
                     continue

from contextlib import ExitStack

import concourse.mybir as mybir
from concourse.masks import make_identity

B, H, H2, D_OUT = 8192, 512, 1024, 128
P = 128
T = 4
EPS = 1e-5
FLOPS = 2 * B * H * H + 2 * B * H2 * D_OUT
SIZES = [2] + [4] * 15 + [2]

F32 = mybir.dt.float32
BF16 = mybir.dt.bfloat16
U32 = mybir.dt.uint32
U8 = mybir.dt.uint8
FP8 = mybir.dt.float8_e4m3fn
FP8X4 = mybir.dt.float8_e4m3fn_x4
ACT = mybir.ActivationFunctionType
ALU = mybir.AluOpType


def tile_rnnclassifier_pa_t_kernel(tc, h1_bytes, h1_scale, W_ih1, b_ih1, b_hh1, ln_g, ln_b, fc_W, fc_b, out):
    nc = tc.nc
    first = [sum(SIZES[:c]) * P for c in range(len(SIZES))]
    nch = len(SIZES)

    def rows(ap, c):
        n = SIZES[c]
        return ap[first[c] : first[c] + n * P, :].rearrange("(q j) k -> q j k", j=n)

    with ExitStack() as ctx:
        const = ctx.enter_context(tc.tile_pool(name="const", bufs=1))
        work = ctx.enter_context(tc.tile_pool(name="work", bufs=2))
        stat = ctx.enter_context(tc.tile_pool(name="stat", bufs=4))
        ps_a = ctx.enter_context(tc.psum_pool(name="ps_a", bufs=2))
        ps_s = ctx.enter_context(tc.psum_pool(name="ps_s", bufs=3))
        ps_f = ctx.enter_context(tc.psum_pool(name="ps_f", bufs=3))

        xb, hx, xg, xc, xs = {}, {}, {}, {}, {}
        hb, hh, zz, sm, nm, sq, rs, nb = {}, {}, {}, {}, {}, {}, {}, {}
        mv = {}
        yy, yg, yc, ys = {}, {}, {}, {}
        osb, fmb, xtb, s1b, ob = {}, {}, {}, {}, {}

        def load(c):
            xb[c] = work.tile([P, 4, H], U8, name="x_bytes", align_bytes=64, bufs=6)
            nc.sync.dma_start(out=xb[c][:, : SIZES[c], :], in_=rows(h1_bytes, c))

        row_b = const.tile([P, H], BF16)
        nc.vector.memset(row_b[:], 0.0)
        row_f = const.tile([P, D_OUT], BF16)
        nc.vector.memset(row_f[:], 0.0)
        ones = const.tile([P, P], BF16)
        nc.vector.memset(ones[:], 1.0)
        ident = const.tile([P, P], F32)
        make_identity(nc, ident[:])
        half = const.tile([P, 4], F32)
        nc.gpsimd.memset(half[:], -0.5)
        dummy = const.tile([P, 1], F32)
        nc.gpsimd.memset(dummy[:], 0.0)

        load(0)
        scale = const.tile([P, 2, H], F32)
        nc.sync.dma_start(out=scale[:, 0, :], in_=h1_scale.rearrange("o k -> (o k)").partition_broadcast(P))
        w_sb = const.tile([P, T, H], BF16)
        nc.sync.dma_start(out=w_sb[:], in_=W_ih1.rearrange("(m t) k -> m t k", t=T))
        nc.scalar.dma_start(out=row_b[0:1, :], in_=b_ih1.rearrange("(o k) -> o k", o=1))
        nc.scalar.dma_start(out=row_b[1:2, :], in_=b_hh1.rearrange("(o k) -> o k", o=1))
        load(1)
        f_sb = const.tile([P, H2], BF16)
        nc.sync.dma_start(out=f_sb[:], in_=fc_W)
        g_raw = const.tile([P, 2, T], BF16)
        nc.gpsimd.dma_start(out=g_raw[:], in_=ln_g.rearrange("(o p t) -> p o t", o=2, t=T))
        b_raw = const.tile([P, 2, T], BF16)
        nc.gpsimd.dma_start(out=b_raw[:], in_=ln_b.rearrange("(o p t) -> p o t", o=2, t=T))
        nc.gpsimd.dma_start(out=row_f[0:1, :], in_=fc_b.rearrange("(o k) -> o k", o=1))
        nc.scalar.activation(out=dummy[:], in_=dummy[:], func=ACT.Tanh)
        nc.scalar.copy(out=scale[:, 1, :], in_=scale[:, 0, :])
        bias = const.tile([P, H], F32)
        g_col = const.tile([P, 2, T], F32)
        b_col = const.tile([P, 2, T], F32)
        fcb = const.tile([P, 4, D_OUT], F32)

        w_grp = const.tile([P, H, T], BF16, align_bytes=64)
        w_codes = const.tile([P, H], U32, align_bytes=64)
        w_scales = const.tile([P, H], U8, align_bytes=64)
        f_grp = const.tile([P, 2 * D_OUT, T], BF16, align_bytes=64)
        f_codes = const.tile([P, 2 * D_OUT], U32, align_bytes=64)
        f_scales = const.tile([P, 2 * D_OUT], U8, align_bytes=64)

        def words(ap):
            return ap.bitcast(F32)

        def a1(c, h):
            if c not in hx:
                hx[c] = work.tile([P, 4, H], BF16, name="hx", align_bytes=64, bufs=3)
            n = min(2, SIZES[c] - 2 * h)
            dst = hx[c][:, 2 * h : 2 * h + n, :].rearrange("p j k -> p (j k)")
            code = xb[c][:, 2 * h : 2 * h + n, :].rearrange("p j k -> p (j k)").bitcast(FP8)
            if c == 0:
                for j in range(2 * h, 2 * h + n):
                    nc.vector.tensor_tensor(out=hx[c][:, j, :], in0=xb[c][:, j, :].bitcast(FP8), in1=scale[:, 0, :], op=ALU.mult)
                return
            nc.vector.tensor_tensor(out=dst, in0=code, in1=scale[:, :n, :].rearrange("p a k -> p (a k)"), op=ALU.mult)

        def a2p(c, h):
            n = min(2, SIZES[c] - 2 * h)
            xtb[c, h] = ps_a.tile([P, 2, 2, P], F32, name="xt")
            for jj in range(n):
                w = words(hx[c][:, 2 * h + jj, :])
                for u in range(2):
                    nc.tensor.transpose(xtb[c, h][:, jj, u, :], w[:, u : H // 2 : 2], ident[:])

        def a2s(c, h):
            if c not in xg:
                xg[c] = work.tile([P, 4 * P, T], BF16, name="xg", align_bytes=64, bufs=3)
            n = min(2, SIZES[c] - 2 * h)
            dst = words(xg[c][:, h * 256 : h * 256 + n * P, :]).rearrange("p (j r) u -> p j r u", j=n)
            nc.scalar.copy(out=dst, in_=xtb[c, h][:, :n].rearrange("p j u r -> p j r u"))

        def a3(c):
            n = SIZES[c] * P
            xc[c] = work.tile([P, 4 * P], U32, name="xc", align_bytes=64, bufs=4)
            xs[c] = work.tile([P, 4 * P], U8, name="xs", align_bytes=64, bufs=4)
            nc.vector.quantize_mx(out=xc[c][:, :n].bitcast(FP8X4), scales=xs[c][:, :n], in_=xg[c][:, :n, :].rearrange("p n t -> p (n t)"))

        def bp(c, j):
            s1b[c, j] = ps_s.tile([P, H], F32, name="s1")
            nc.tensor.matmul_mx(
                out=s1b[c, j][:],
                lhsT=xc[c][:, j * P : (j + 1) * P].bitcast(FP8X4),
                lhsT_scale=xs[c][:, j * P : (j + 1) * P],
                rhs=w_codes[:].bitcast(FP8X4),
                rhs_scale=w_scales[:],
                start=True,
                stop=True,
            )

        def bv(c, j):
            hb[c, j] = work.tile([P, H], F32, name="hb", bufs=4)
            nc.vector.tensor_tensor(out=hb[c, j][:], in0=s1b[c, j][:], in1=bias[:], op=ALU.add)

        def bs(c, j):
            if c not in hh:
                hh[c] = work.tile([P, 4, H], F32, name="hh", bufs=3)
                sm[c] = stat.tile([P, 4], F32, name="sm")
                nm[c] = stat.tile([P, 4], F32, name="nm")
                sq[c] = stat.tile([P, 4], F32, name="sq")
                rs[c] = stat.tile([P, 4], F32, name="rs")
            nc.scalar.activation(out=hh[c][:, j, :], in_=hb[c, j][:], func=ACT.Tanh, accum_out=sm[c][:, j : j + 1])

        def cgN(c):
            n = SIZES[c]
            nc.gpsimd.tensor_scalar(out=nm[c][:, :n], in0=sm[c][:, :n], scalar1=-1.0 / H, scalar2=0.0, op0=ALU.mult, op1=ALU.add)

        def cq(c, j):
            junk = work.tile([P, H], BF16, name="junk", bufs=2)
            nc.scalar.activation(out=junk[:], in_=hh[c][:, j, :], func=ACT.Square, scale=-float(H), bias=sm[c][:, j : j + 1], accum_out=sq[c][:, j : j + 1])

        def cgA(c):
            n = SIZES[c]
            nc.gpsimd.tensor_scalar(out=rs[c][:, :n], in0=sq[c][:, :n], scalar1=1.0 / H**3, scalar2=EPS, op0=ALU.mult, op1=ALU.add)

        def cgP(c):
            n = SIZES[c]
            nc.gpsimd.tensor_tensor(out=rs[c][:, :n], in0=rs[c][:, :n], in1=half[:, :n], op=ALU.pow)

        def cs(c, j):
            if c not in zz:
                zz[c] = work.tile([P, 4, H], F32, name="zz", bufs=3)
            eng = nc.gpsimd if "GVGV"[j] == "G" else nc.vector
            eng.tensor_scalar(
                out=zz[c][:, j, :], in0=hh[c][:, j, :], scalar1=nm[c][:, j : j + 1], scalar2=rs[c][:, j : j + 1], op0=ALU.add, op1=ALU.mult
            )

        def dp(c, t):
            fmb[c, t] = ps_f.tile([P, 4 * P], F32, name="fm")
            for j in range(SIZES[c]):
                nc.tensor.transpose(fmb[c, t][:, j * P : (j + 1) * P], zz[c][:, j, t * P : (t + 1) * P], ident[:])

        affine_on_vector = {"even": [], "odd": [(3, 1)], "last": []}

        def ds(c, t, o):
            n = SIZES[c] * P
            if (c, o) not in yy:
                yy[c, o] = work.tile([P, T, 4 * P], BF16, name="yy%d" % o, bufs=3)
            dst, src = yy[c, o][:, t, :n], fmb[c, t][:, :n]
            scl, sft = g_col[:, o, t : t + 1], b_col[:, o, t : t + 1]
            if (t, o) in affine_on_vector["last" if c == nch - 1 else ("odd" if c % 2 else "even")]:
                nc.vector.tensor_scalar(out=dst, in0=src, scalar1=scl, scalar2=sft, op0=ALU.mult, op1=ALU.add)
            else:
                nc.scalar.activation(out=dst, in_=src, func=ACT.Identity, scale=scl, bias=sft)

        parts = [[4],[4]]

        def e1(c, o, part):
            if (c, o) not in yg:
                yg[c, o] = work.tile([P, 4 * P, T], BF16, name="yg%d" % o, align_bytes=64, bufs=3)
            a = sum(parts[o][:part]) * 32 * SIZES[c]
            ns = slice(a, a + parts[o][part] * 32 * SIZES[c])
            nc.vector.tensor_copy(
                out=yg[c, o][:, ns, :].rearrange("p (n i) t -> p n t i", i=4),
                in_=yy[c, o][:, :, ns].rearrange("p t (n i) -> p n t i", i=4),
            )

        def e2(c, o):
            n = SIZES[c] * P
            yc[c, o] = work.tile([P, 4 * P], U32, name="yc%d" % o, align_bytes=64, bufs=3)
            ys[c, o] = work.tile([P, 4 * P], U8, name="ys%d" % o, align_bytes=64, bufs=3)
            nc.vector.quantize_mx(out=yc[c, o][:, :n].bitcast(FP8X4), scales=ys[c, o][:, :n], in_=yg[c, o][:, :n, :].rearrange("p n t -> p (n t)"))

        def fp(c):
            xo = ps_a.tile([P, 2, 2, P], F32, name="xt")
            ob[c] = xo[:].rearrange("p a b r -> p (a b) r")
            for j in range(SIZES[c]):
                for o in range(2):
                    nc.tensor.matmul_mx(
                        out=ob[c][:, j, :],
                        lhsT=yc[c, o][:, j * P : (j + 1) * P].bitcast(FP8X4),
                        lhsT_scale=ys[c, o][:, j * P : (j + 1) * P],
                        rhs=f_codes[:, o * P : (o + 1) * P].bitcast(FP8X4),
                        rhs_scale=f_scales[:, o * P : (o + 1) * P],
                        start=(o == 0),
                        stop=(o == 1),
                    )

        def fv(c):
            n = SIZES[c]
            osb[c] = work.tile([P, 4, D_OUT], F32, name="osb", bufs=3)
            nc.vector.tensor_tensor(out=osb[c][:, :n, :], in0=ob[c][:, :n, :], in1=fcb[:, :n, :], op=ALU.add)

        def st_out(c):
            nc.sync.dma_start(out=rows(out, c), in_=osb[c][:, : SIZES[c], :])

        def turn_weights(src, pieces, grp):
            xt = ps_f.tile([P, 4 * P], F32, name="fm")
            v = xt[:].rearrange("p (a u r) -> p a u r", a=2, u=2)
            for a in range(2):
                for u in range(2):
                    nc.tensor.transpose(v[:, a, u, :], pieces[a][:, u : H // 2 : 2], ident[:])
            nc.scalar.copy(out=words(grp).rearrange("p (j r) u -> p j r u", j=2), in_=v.rearrange("p j u r -> p j r u"))

        def weights():
            for h in range(2):
                turn_weights(None, [words(w_sb[:, 2 * h + a, :]) for a in range(2)], w_grp[:, h * 256 : h * 256 + 256, :])
        def weights_quantised():
            nc.vector.quantize_mx(out=w_codes[:].bitcast(FP8X4), scales=w_scales[:], in_=w_grp[:].rearrange("p n t -> p (n t)"))

        def small_constants():
            bk = ps_f.tile([P, 4 * P], F32, name="fm")
            nc.tensor.matmul(bk[:], lhsT=ones[:], rhs=row_b[:], start=True, stop=True)
            nc.scalar.copy(out=bias[:].rearrange("p (t m) -> p t m", t=T), in_=bk[:].rearrange("p (m t) -> p t m", t=T))

        def late_constants():
            nc.gpsimd.tensor_copy(out=g_col[:], in_=g_raw[:])
            nc.gpsimd.tensor_copy(out=b_col[:], in_=b_raw[:])
            fk = ps_f.tile([P, 4 * P], F32, name="fm")
            for j in range(4):
                nc.tensor.matmul(fk[:, j * P : (j + 1) * P], lhsT=ones[:], rhs=row_f[:], start=True, stop=True)
            nc.scalar.copy(out=fcb[:].rearrange("p j f -> p (j f)"), in_=fk[:])
            fw = words(f_sb[:])
            turn_weights(None, [fw[:, 256 * o : 256 * (o + 1)] for o in range(2)], f_grp[:])
            nc.vector.quantize_mx(out=f_codes[:].bitcast(FP8X4), scales=f_scales[:], in_=f_grp[:].rearrange("p n t -> p (n t)"))

        steps = [
            (e2, (0,), 6),
            (dp, (3,), 5),
            (cgP, (), 4),
            (a2p, (1,), 1),
            (load, (), 0),
            (bp, (2,), 3),
            (ds, (2, 1), 5),
            (a2s, (0,), 1),
            (ds, (1, 1), 5),
            (ds, (2, 0), 5),
            (bv, (3,), 3),
            (cs, (2,), 4),
            (ds, (3, 1), 5),
            (ds, (1, 0), 5),
            (bv, (2,), 3),
            (bp, (0,), 2),
            (bs, (0,), 3),
            (ds, (3, 0), 5),
            (a2s, (1,), 1),
            (bs, (1,), 3),
            (cs, (1,), 4),
            (a1, (0,), 0),
            (bp, (3,), 2),
            (cq, (0,), 3),
            (cs, (3,), 4),
            (bs, (3,), 3),
            (cq, (1,), 3),
            (cs, (0,), 4),
            (e1, (1, 0), 5),
            (e1, (0, 0), 5),
            (a1, (1,), 0),
            (dp, (0,), 4),
            (fp, (), 6),
            (bs, (2,), 3),
            (dp, (2,), 4),
            (a2p, (0,), 0),
            (e2, (1,), 5),
            (bv, (0,), 2),
            (cq, (3,), 3),
            (cq, (2,), 3),
            (ds, (0, 1), 4),
            (a3, (), 1),
            (bp, (1,), 2),
            (fv, (), 6),
            (bv, (1,), 2),
            (ds, (0, 0), 4),
            (st_out, (), 6),
            (dp, (1,), 4),
            (cgN, (), 3),
            (cgA, (), 3),
        ]
        ctx.enter_context(tc.manual_schedule())
        a1(0, 0)
        a2p(0, 0)
        a2s(0, 0)
        a1(1, 0)
        a3(0)
        weights()
        weights_quantised()
        small_constants()
        early = [(a1, 0, 0), (a2p, 0, 0), (a2s, 0, 0), (a3, 0), (a1, 1, 0)]
        for i in range(nch + 7):
            for fn, args, lag in steps:
                c = i - lag
                if not 0 <= c < nch or (fn, c, *args) in early or (fn is load and c <= 1):
                    continue
                if fn in (a1, a2p, a2s) and 2 * args[0] >= SIZES[c] or fn in (bp, bv, bs, cq, cs) and args[0] >= SIZES[c]:
                    continue
                fn(c, *args)
            if i == 1:
                late_constants()
